import numpy as np
import ml_dtypes


def mxq(x, axis, fmt="e4m3"):
    dtype, down = {"e4m3": (ml_dtypes.float8_e4m3fn, 7), "e5m2": (ml_dtypes.float8_e5m2, 14)}[fmt]
    v = np.moveaxis(np.asarray(x, np.float32).astype(ml_dtypes.bfloat16).astype(np.float64), axis, -1)
    blocks = v.reshape(v.shape[:-1] + (-1, 32))
    amax = np.abs(blocks).max(-1, keepdims=True)
    byte = np.maximum(np.where(amax > 0, np.frexp(amax)[1] - 1 + 127, 0) - down, 1)
    scale = np.exp2(byte - 127.0)
    codes = (blocks / scale).astype(np.float32).astype(dtype).astype(np.float64)
    return np.moveaxis((codes * scale).reshape(v.shape), -1, axis)


WIDE = False


def mx_kscale(k):
    if not WIDE:
        return np.ones(k)
    levels = np.array([10, -10, 5, -5, 0])
    a = np.random.permutation(np.resize(levels, k // 512 * 4)).reshape(k // 512, 4)
    idx = np.arange(k)
    return np.exp2(a[idx // 512, idx % 128 // 32])


BF16 = ml_dtypes.bfloat16


def bf(x):
    return np.asarray(x, np.float32).astype(BF16)


def f64(x):
    return np.asarray(x).astype(np.float64)


E2M1 = np.array([0.0, 0.5, 1.0, 1.5, 2.0, 3.0, 4.0, 6.0, -0.0, -0.5, -1.0, -1.5, -2.0, -3.0, -4.0, -6.0])


def pack_weight(w, fmt):
    k, n = w.shape
    w = f64(bf(w)).reshape(k // 32, 32, n)
    amax = np.abs(w).max(1)
    if fmt == "e4m3":
        byte = np.frexp(amax)[1] - 1 + 127 - 7
    else:
        mant, ex = np.frexp(amax / 6.0)
        byte = np.where(mant > 0.5, ex, ex - 1) + 127
    byte = np.clip(np.where(amax > 0, byte, 1), 1, 254)
    scaled = (w * np.exp2(127.0 - byte)[:, None, :]).reshape(k, n).astype(np.float32)
    by_word = np.ascontiguousarray(scaled.reshape(k // 512, 128, 4, n).transpose(0, 1, 3, 2))
    if fmt == "e4m3":
        words = by_word.astype(ml_dtypes.float8_e4m3fn).view(np.uint8)
    else:
        c = by_word.astype(ml_dtypes.float4_e2m1fn).view(np.uint8) & 0xF
        words = c[..., 0::2] | (c[..., 1::2] << 4)
    return np.ascontiguousarray(words), np.ascontiguousarray(byte.astype(np.uint8).reshape(k // 512, 16, n))


def unpack_weight(words, scales, fmt):
    g, p, n, _ = words.shape
    if fmt == "e4m3":
        vals = np.ascontiguousarray(words).view(ml_dtypes.float8_e4m3fn).astype(np.float64)
    else:
        nib = np.empty((g, p, n, 4), np.uint8)
        nib[..., 0::2] = words & 0xF
        nib[..., 1::2] = words >> 4
        vals = E2M1[nib]
    vals = vals * np.repeat(np.exp2(scales.astype(np.float64) - 127.0), 8, axis=1)[..., None]
    return vals.transpose(0, 1, 3, 2).reshape(g * 512, n)

def pack4(w):
    words, scales = pack_weight(w, "e2m1")
    return words.reshape(words.shape[0], 128, -1), scales


def unpack4(words, scales):
    return unpack_weight(words.reshape(words.shape[0], 128, -1, 2), scales, "e2m1")


B, S, E, N_HEAD, MP_NUM, ROTARY_DIM = 2, 128, 512, 16, 4, 16
HEAD_DIM = E // N_HEAD
LOCAL = E // MP_NUM
ROPE_BASE = 10000.0


def rotate_every_two(x):
    x1 = x[..., 0::2]
    x2 = x[..., 1::2]
    return np.stack((-x2, x1), axis=-1).reshape(x.shape)


def rope(x, sin, cos):
    x_rot = x[..., :ROTARY_DIM]
    x_pass = x[..., ROTARY_DIM:]
    x_rot = x_rot * cos + rotate_every_two(x_rot) * sin
    return np.concatenate([x_rot, x_pass], axis=-1)


def setup_inputs():
    s = mx_kscale(E)
    hidden_states = bf(np.random.standard_normal((B, S, E)) * s)
    w = np.random.standard_normal((3 * E, E)) / np.sqrt(E) / s[None, :]
    words, scales = pack4(w.T)
    return {"hidden_states": hidden_states,
            "w_qkv_words": words,
            "w_qkv_scales": scales}


def reference(hidden_states, w_qkv_words, w_qkv_scales):
    qkv = mxq(f64(hidden_states), 2, "e4m3") @ unpack4(w_qkv_words, w_qkv_scales)
    qkv = qkv.reshape(B, S, MP_NUM, 3 * LOCAL)
    q = qkv[..., :LOCAL].reshape(B, S, N_HEAD, HEAD_DIM)
    v = qkv[..., LOCAL:2 * LOCAL].reshape(B, S, N_HEAD, HEAD_DIM)
    k = qkv[..., 2 * LOCAL:].reshape(B, S, N_HEAD, HEAD_DIM)
    inv_freq = 1.0 / (ROPE_BASE ** (np.arange(0, ROTARY_DIM, 2) / ROTARY_DIM))
    freqs = np.arange(S)[:, None] * inv_freq[None, :]
    sin = np.repeat(np.sin(freqs), 2, axis=-1)[None, :, None, :]
    cos = np.repeat(np.cos(freqs), 2, axis=-1)[None, :, None, :]
    q = rope(q, sin, cos)
    k = rope(k, sin, cos)
    return q.transpose(0, 2, 1, 3), k.transpose(0, 2, 1, 3), v.transpose(0, 2, 1, 3)

@@ -1,0 +1,190 @@
+import math
+from contextlib import ExitStack
+
+import concourse.mybir as mybir
+from concourse.masks import make_identity
+
+F32 = mybir.dt.float32
+BF16 = mybir.dt.bfloat16
+I32 = mybir.dt.int32
+U32 = mybir.dt.uint32
+U8 = mybir.dt.uint8
+FP8X4 = mybir.dt.float8_e4m3fn_x4
+FP4X4 = mybir.dt.float4_e2m1fn_x4
+ALU = mybir.AluOpType
+ACT = mybir.ActivationFunctionType
+
+P = 128
+BATCH, SEQ, E = 2, 128, 512
+HEADS, HEAD_DIM, ROTARY_DIM = 16, 32, 16
+ROT_PAIRS = ROTARY_DIM // 2
+ROPE_BASE = 10000.0
+SHARDS = 4
+BLOCK = 128
+QUERY, VALUE, KEY = 0, 1, 2
+PACK = 4
+SCALE_ROWS = 4
+
+FLOPS = 2 * BATCH * SEQ * E * 3 * E
+
+ROUND = 12582912.0
+
+SINE_FORM = (((1.0, 0.25), (1.0, 0.0)), ((-1.0, 0.0), (1.0, 0.25)))
+
+
+def tile_ttcodegenattention_pa_s_kernel(
+    tc, hidden_states, w_qkv_words, w_qkv_scales, out_0, out_1, out_2
+):
+    nc = tc.nc
+    with ExitStack() as ctx:
+        keep = ctx.enter_context(tc.tile_pool(name="keep", bufs=1))
+        psum = ctx.enter_context(tc.psum_pool(name="psum", bufs=1))
+        ctx.enter_context(tc.manual_schedule())
+
+        x_sb = keep.tile([P, 2, E], BF16)
+        x_by_par = hidden_states.rearrange("b (pair par) k -> par pair b k", par=2)
+        for par in range(2):
+            nc.sync.dma_start(out=x_sb[:, par, :], in_=x_by_par[par])
+
+        w_scales = keep.tile([P, 3 * E], U8, align_bytes=64)
+        nc.vector.memset(w_scales[:].bitcast(I32), 0)
+        for quadrant in range(4):
+            nc.sync.dma_start(
+                out=w_scales[32 * quadrant : 32 * quadrant + SCALE_ROWS, :].bitcast(I32),
+                in_=w_qkv_scales[0, SCALE_ROWS * quadrant : SCALE_ROWS * (quadrant + 1), :].bitcast(I32),
+            )
+        w_words = keep.tile([P, 2 * 3 * E], U8, align_bytes=64)
+        nc.sync.dma_start(out=w_words[:].bitcast(I32), in_=w_qkv_words[0].bitcast(I32))
+
+        warm = keep.tile([P, 1], F32)
+        nc.vector.memset(warm[:], 0.0)
+        nc.scalar.activation(out=warm[:], in_=warm[:], func=ACT.Sin)
+
+        lane = keep.tile([P, 2], I32)
+        nc.gpsimd.iota(lane[:], pattern=[[0, 2]], base=0, channel_multiplier=1)
+        par_bit = keep.tile([P, 2], I32)
+        nc.gpsimd.iota(par_bit[:], pattern=[[1, 2]], base=0, channel_multiplier=0)
+        identity = keep.tile([P, P], F32)
+        make_identity(nc, identity[:])
+
+        even_pos = keep.tile([P, 2], I32)
+        nc.vector.tensor_single_scalar(out=even_pos[:], in_=lane[:], scalar=P - 2, op=ALU.bitwise_and)
+        pos = keep.tile([P, 2], F32)
+        nc.vector.tensor_tensor(out=pos[:], in0=even_pos[:], in1=par_bit[:], op=ALU.add)
+        turns = keep.tile([P, 2, ROT_PAIRS], F32)
+        for i in range(ROT_PAIRS):
+            per_position = 1.0 / (ROPE_BASE ** (2.0 * i / ROTARY_DIM)) / (2.0 * math.pi)
+            nc.vector.tensor_scalar_mul(out=turns[:, :, i], in0=pos[:], scalar1=per_position)
+        phase = keep.tile([P, 2, 2, ROT_PAIRS, 2], F32)
+        for src in range(2):
+            for dst in range(2):
+                sign, shift = SINE_FORM[src][dst]
+                nc.vector.tensor_scalar(
+                    out=phase[:, :, src, :, dst],
+                    in0=turns[:],
+                    scalar1=sign,
+                    scalar2=shift,
+                    op0=ALU.mult,
+                    op1=ALU.add,
+                )
+        phase_flat = phase[:].rearrange("p par src i dst -> p (par src i dst)")
+        whole = keep.tile([P, 2 * 2 * ROTARY_DIM], F32)
+        nc.vector.tensor_scalar(
+            out=whole[:], in0=phase_flat, scalar1=ROUND, scalar2=ROUND, op0=ALU.add, op1=ALU.subtract
+        )
+        part = keep.tile([P, 2 * 2 * ROTARY_DIM], F32)
+        nc.vector.tensor_tensor(out=part[:], in0=phase_flat, in1=whole[:], op=ALU.subtract)
+
+        x_grouped = keep.tile([P, 2, P, PACK], BF16, align_bytes=64)
+        x_codes = keep.tile([P, 2, P], U32, align_bytes=64)
+        x_scales = keep.tile([P, 2, P], U8, align_bytes=64)
+        for par in range(2):
+            x_words = x_sb[:, par, :].bitcast(F32)
+            x_t = psum.tile([P, 2, P], F32, name="x_t%d" % par)
+            for u in range(2):
+                nc.tensor.transpose(x_t[:, u, :], x_words[:, u : E // 2 : 2], identity[:])
+            nc.scalar.copy(
+                out=x_grouped[:, par]
+                .rearrange("p m t -> p (m t)")
+                .bitcast(F32)
+                .rearrange("p (m u) -> p m u", u=2),
+                in_=x_t[:].rearrange("p u m -> p m u"),
+            )
+        for par in range(2):
+            nc.vector.quantize_mx(
+                out=x_codes[:, par, :].bitcast(FP8X4),
+                scales=x_scales[:, par, :],
+                in_=x_grouped[:, par].rearrange("p m t -> p (m t)"),
+            )
+        factor = keep.tile([P, 2, 2, ROT_PAIRS, 2], F32)
+        nc.scalar.activation(
+            out=factor[:].rearrange("p par src i dst -> p (par src i dst)"),
+            in_=part[:],
+            func=ACT.Sin,
+            scale=2.0 * math.pi,
+        )
+
+        def project(kind, name):
+            banks = []
+            for par in range(2):
+                bank = psum.tile([P, SHARDS, BLOCK], F32, name="%s%d" % (name, par))
+                for shard in range(SHARDS):
+                    col = (3 * shard + kind) * BLOCK
+                    nc.tensor.matmul_mx(
+                        out=bank[:, shard, :],
+                        lhsT=x_codes[:, par, :].bitcast(FP8X4),
+                        lhsT_scale=x_scales[:, par, :],
+                        rhs=w_words[:, 2 * col : 2 * (col + BLOCK)].bitcast(FP4X4),
+                        rhs_scale=w_scales[:, col : col + BLOCK],
+                        start=True,
+                        stop=True,
+                    )
+                banks.append(bank)
+            return banks
+
+        v_banks = project(VALUE, "v_ps")
+        q_banks = project(QUERY, "q_ps")
+        k_banks = project(KEY, "k_ps")
+
+        def by_head(bank):
+            return bank[:].rearrange("p shard (h d) -> p (shard h) d", d=HEAD_DIM)
+
+        def store(out, result):
+            for b in range(BATCH):
+                nc.sync.dma_start(
+                    out=out[b].rearrange("h (pair par) d -> pair h (par d)", par=2),
+                    in_=result[b:P:BATCH].rearrange("p h par d -> p h (par d)"),
+                )
+
+        v_sb = keep.tile([P, HEADS, 2, HEAD_DIM], F32)
+        nc.scalar.copy(out=v_sb[:, :, 0, :], in_=by_head(v_banks[0]))
+        nc.vector.tensor_copy(out=v_sb[:, :, 1, :], in_=by_head(v_banks[1]))
+        store(out_2, v_sb)
+
+        def rotate(banks, name, out):
+            result = keep.tile([P, HEADS, 2, HEAD_DIM], F32, name=name)
+            from_src = [
+                keep.tile([P, HEADS, 2, ROT_PAIRS, 2], F32, name="%s_from%d" % (name, src))
+                for src in range(2)
+            ]
+            shape = [P, HEADS, ROT_PAIRS, 2]
+            for par in range(2):
+                nc.scalar.copy(out=result[:, :, par, :], in_=by_head(banks[par]))
+                pairs = result[:, :, par, 0:ROTARY_DIM].rearrange("p h (i e) -> p h i e", e=2)
+                for src in range(2):
+                    nc.vector.tensor_tensor(
+                        out=from_src[src][:, :, par],
+                        in0=pairs[:, :, :, src : src + 1].to_broadcast(shape),
+                        in1=factor[:, par, src].unsqueeze(1).to_broadcast(shape),
+                        op=ALU.mult,
+                    )
+            nc.vector.tensor_tensor(
+                out=result[:, :, :, 0:ROTARY_DIM],
+                in0=from_src[0][:].rearrange("p h par i e -> p h par (i e)"),
+                in1=from_src[1][:].rearrange("p h par i e -> p h par (i e)"),
+                op=ALU.add,
+            )
+            store(out, result)
+
+        rotate(q_banks, "q_sb", out_0)
+        rotate(k_banks, "k_sb", out_1)

@@ -16,12 +16,13 @@ ACT = mybir.ActivationFunctionType
 
 P = 128
 BATCH, SEQ, E = 2, 128, 512
-HEADS, HEAD_DIM, ROTARY_DIM = 16, 32, 16
+HEAD_DIM, ROTARY_DIM = 32, 16
 ROT_PAIRS = ROTARY_DIM // 2
 ROPE_BASE = 10000.0
-SHARDS = 4
 BLOCK = 128
 QUERY, VALUE, KEY = 0, 1, 2
+UNIT_SHARDS = 2
+UNIT_HEADS = UNIT_SHARDS * BLOCK // HEAD_DIM
 PACK = 4
 SCALE_ROWS = 4
 
@@ -124,14 +125,13 @@ def tile_ttcodegenattention_pa_s_kernel(
             scale=2.0 * math.pi,
         )
 
-        def project(kind, name):
-            banks = []
+        def project(kind, half, name):
+            bank = psum.tile([P, 2, UNIT_SHARDS, BLOCK], F32, name=name)
             for par in range(2):
-                bank = psum.tile([P, SHARDS, BLOCK], F32, name="%s%d" % (name, par))
-                for shard in range(SHARDS):
-                    col = (3 * shard + kind) * BLOCK
+                for s in range(UNIT_SHARDS):
+                    col = (3 * (UNIT_SHARDS * half + s) + kind) * BLOCK
                     nc.tensor.matmul_mx(
-                        out=bank[:, shard, :],
+                        out=bank[:, par, s, :],
                         lhsT=x_codes[:, par, :].bitcast(FP8X4),
                         lhsT_scale=x_scales[:, par, :],
                         rhs=w_words[:, 2 * col : 2 * (col + BLOCK)].bitcast(FP4X4),
@@ -139,52 +139,47 @@ def tile_ttcodegenattention_pa_s_kernel(
                         start=True,
                         stop=True,
                     )
-                banks.append(bank)
-            return banks
+            return bank
 
-        v_banks = project(VALUE, "v_ps")
-        q_banks = project(QUERY, "q_ps")
-        k_banks = project(KEY, "k_ps")
+        banks = {}
+        for kind in (VALUE, QUERY, KEY):
+            for half in range(2):
+                banks[(kind, half)] = project(kind, half, "bank_%d_%d" % (kind, half))
 
-        def by_head(bank):
-            return bank[:].rearrange("p shard (h d) -> p (shard h) d", d=HEAD_DIM)
+        def empty(copy, bank, name):
+            result = keep.tile([P, UNIT_HEADS, 2, HEAD_DIM], F32, name=name)
+            copy(
+                out=result[:].rearrange("p h par d -> p par h d"),
+                in_=bank[:].rearrange("p par s (h d) -> p par (s h) d", d=HEAD_DIM),
+            )
+            return result
 
-        def store(out, result):
+        def store(out, half, result):
+            heads = slice(UNIT_HEADS * half, UNIT_HEADS * (half + 1))
             for b in range(BATCH):
                 nc.sync.dma_start(
-                    out=out[b].rearrange("h (pair par) d -> pair h (par d)", par=2),
+                    out=out[b, heads].rearrange("h (pair par) d -> pair h (par d)", par=2),
                     in_=result[b:P:BATCH].rearrange("p h par d -> p h (par d)"),
                 )
 
-        v_sb = keep.tile([P, HEADS, 2, HEAD_DIM], F32)
-        nc.scalar.copy(out=v_sb[:, :, 0, :], in_=by_head(v_banks[0]))
-        nc.vector.tensor_copy(out=v_sb[:, :, 1, :], in_=by_head(v_banks[1]))
-        store(out_2, v_sb)
+        store(out_2, 0, empty(nc.scalar.copy, banks[(VALUE, 0)], "v_0"))
+        store(out_2, 1, empty(nc.vector.tensor_copy, banks[(VALUE, 1)], "v_1"))
 
-        def rotate(banks, name, out):
-            result = keep.tile([P, HEADS, 2, HEAD_DIM], F32, name=name)
-            from_src = [
-                keep.tile([P, HEADS, 2, ROT_PAIRS, 2], F32, name="%s_from%d" % (name, src))
-                for src in range(2)
-            ]
-            shape = [P, HEADS, ROT_PAIRS, 2]
-            for par in range(2):
-                nc.scalar.copy(out=result[:, :, par, :], in_=by_head(banks[par]))
-                pairs = result[:, :, par, 0:ROTARY_DIM].rearrange("p h (i e) -> p h i e", e=2)
+        shape = [P, UNIT_HEADS, 2, ROT_PAIRS, 2]
+        for kind, out in ((QUERY, out_0), (KEY, out_1)):
+            for half in range(2):
+                result = empty(nc.scalar.copy, banks[(kind, half)], "qk_%d_%d" % (kind, half))
+                rotary = result[:, :, :, 0:ROTARY_DIM]
+                pairs = rotary.rearrange("p h par (i e) -> p h par i e", e=2)
+                from_src = []
                 for src in range(2):
+                    share = keep.tile(shape, F32, name="from_%d_%d_%d" % (src, kind, half))
                     nc.vector.tensor_tensor(
-                        out=from_src[src][:, :, par],
-                        in0=pairs[:, :, :, src : src + 1].to_broadcast(shape),
-                        in1=factor[:, par, src].unsqueeze(1).to_broadcast(shape),
+                        out=share[:],
+                        in0=pairs[:, :, :, :, src : src + 1].to_broadcast(shape),
+                        in1=factor[:, :, src].unsqueeze(1).to_broadcast(shape),
                         op=ALU.mult,
                     )
-            nc.vector.tensor_tensor(
-                out=result[:, :, :, 0:ROTARY_DIM],
-                in0=from_src[0][:].rearrange("p h par i e -> p h par (i e)"),
-                in1=from_src[1][:].rearrange("p h par i e -> p h par (i e)"),
-                op=ALU.add,
-            )
-            store(out, result)
-
-        rotate(q_banks, "q_sb", out_0)
-        rotate(k_banks, "k_sb", out_1)
+                    from_src.append(share[:].rearrange("p h par i e -> p h par (i e)"))
+                nc.vector.tensor_tensor(out=rotary, in0=from_src[0], in1=from_src[1], op=ALU.add)
+                store(out, half, result)

@@ -165,21 +165,22 @@ def tile_ttcodegenattention_pa_s_kernel(
         store(out_2, 0, empty(nc.scalar.copy, banks[(VALUE, 0)], "v_0"))
         store(out_2, 1, empty(nc.vector.tensor_copy, banks[(VALUE, 1)], "v_1"))
 
-        shape = [P, UNIT_HEADS, 2, ROT_PAIRS, 2]
+        shape = [P, 2, UNIT_HEADS, ROT_PAIRS, 2]
         for kind, out in ((QUERY, out_0), (KEY, out_1)):
             for half in range(2):
-                result = empty(nc.scalar.copy, banks[(kind, half)], "qk_%d_%d" % (kind, half))
+                bank = banks[(kind, half)]
+                result = empty(nc.scalar.copy, bank, "qk_%d_%d" % (kind, half))
                 rotary = result[:, :, :, 0:ROTARY_DIM]
-                pairs = rotary.rearrange("p h par (i e) -> p h par i e", e=2)
-                from_src = []
-                for src in range(2):
-                    share = keep.tile(shape, F32, name="from_%d_%d_%d" % (src, kind, half))
+                odd_share = keep.tile([P, UNIT_HEADS, 2, ROTARY_DIM], F32, name="odd_%d_%d" % (kind, half))
+                pairs = bank[:].rearrange(
+                    "p par s (h r i e) -> p par (s h) r i e", r=HEAD_DIM // ROTARY_DIM, i=ROT_PAIRS, e=2
+                )[:, :, :, 0]
+                for src, share in ((0, rotary), (1, odd_share[:])):
                     nc.vector.tensor_tensor(
-                        out=share[:],
+                        out=share.rearrange("p h par (i e) -> p par h i e", e=2),
                         in0=pairs[:, :, :, :, src : src + 1].to_broadcast(shape),
-                        in1=factor[:, :, src].unsqueeze(1).to_broadcast(shape),
+                        in1=factor[:, :, src].unsqueeze(2).to_broadcast(shape),
                         op=ALU.mult,
                     )
-                    from_src.append(share[:].rearrange("p h par i e -> p h par (i e)"))
-                nc.vector.tensor_tensor(out=rotary, in0=from_src[0], in1=from_src[1], op=ALU.add)
+                nc.gpsimd.tensor_tensor(out=rotary, in0=rotary, in1=odd_share[:], op=ALU.add)
                 store(out, half, result)

@@ -26,6 +26,8 @@ UNIT_HEADS = UNIT_SHARDS * BLOCK // HEAD_DIM
 PACK = 4
 SCALE_ROWS = 4
 
+WARM_BEFORE, WARM_AFTER = 5, 2
+
 FLOPS = 2 * BATCH * SEQ * E * 3 * E
 
 ROUND = 12582912.0
@@ -41,6 +43,16 @@ def tile_ttcodegenattention_pa_s_kernel(
         keep = ctx.enter_context(tc.tile_pool(name="keep", bufs=1))
         psum = ctx.enter_context(tc.psum_pool(name="psum", bufs=1))
         ctx.enter_context(tc.manual_schedule())
+
+        zeros = keep.tile([P, P], F32)
+        nc.gpsimd.memset(zeros[:], 0.0)
+        last_bank = psum.tile([P, 2, UNIT_SHARDS, BLOCK], F32, name="bank_%d_%d" % (KEY, 1))
+
+        def idle_matmuls(count):
+            for unused in range(count):
+                nc.tensor.matmul(out=last_bank[:, 0, 0, :], lhsT=zeros[:], rhs=zeros[:], start=True, stop=True)
+
+        idle_matmuls(WARM_BEFORE)
 
         x_sb = keep.tile([P, 2, E], BF16)
         x_by_par = hidden_states.rearrange("b (pair par) k -> par pair b k", par=2)
@@ -111,6 +123,7 @@ def tile_ttcodegenattention_pa_s_kernel(
                 .rearrange("p (m u) -> p m u", u=2),
                 in_=x_t[:].rearrange("p u m -> p m u"),
             )
+        idle_matmuls(WARM_AFTER)
         for par in range(2):
             nc.vector.quantize_mx(
                 out=x_codes[:, par, :].bitcast(FP8X4),
@@ -126,7 +139,7 @@ def tile_ttcodegenattention_pa_s_kernel(
         )
 
         def project(kind, half, name):
-            bank = psum.tile([P, 2, UNIT_SHARDS, BLOCK], F32, name=name)
+            bank = last_bank if (kind, half) == (KEY, 1) else psum.tile([P, 2, UNIT_SHARDS, BLOCK], F32, name=name)
             for par in range(2):
                 for s in range(UNIT_SHARDS):
                     col = (3 * (UNIT_SHARDS * half + s) + kind) * BLOCK

@@ -182,12 +182,11 @@ def tile_ttcodegenattention_pa_s_kernel(
         for kind, out in ((QUERY, out_0), (KEY, out_1)):
             for half in range(2):
                 bank = banks[(kind, half)]
-                result = empty(nc.scalar.copy, bank, "qk_%d_%d" % (kind, half))
+                result = keep.tile([P, UNIT_HEADS, 2, HEAD_DIM], F32, name="qk_%d_%d" % (kind, half))
                 rotary = result[:, :, :, 0:ROTARY_DIM]
                 odd_share = keep.tile([P, UNIT_HEADS, 2, ROTARY_DIM], F32, name="odd_%d_%d" % (kind, half))
-                pairs = bank[:].rearrange(
-                    "p par s (h r i e) -> p par (s h) r i e", r=HEAD_DIM // ROTARY_DIM, i=ROT_PAIRS, e=2
-                )[:, :, :, 0]
+                heads = bank[:].rearrange("p par s (h d) -> p par (s h) d", d=HEAD_DIM)
+                pairs = heads[:, :, :, 0:ROTARY_DIM].rearrange("p par h (i e) -> p par h i e", e=2)
                 for src, share in ((0, rotary), (1, odd_share[:])):
                     nc.vector.tensor_tensor(
                         out=share.rearrange("p h par (i e) -> p par h i e", e=2),
@@ -195,5 +194,10 @@ def tile_ttcodegenattention_pa_s_kernel(
                         in1=factor[:, :, src].unsqueeze(2).to_broadcast(shape),
                         op=ALU.mult,
                     )
-                nc.gpsimd.tensor_tensor(out=rotary, in0=rotary, in1=odd_share[:], op=ALU.add)
+                nc.scalar.copy(
+                    out=result[:, :, :, ROTARY_DIM:HEAD_DIM].rearrange("p h par d -> p par h d"),
+                    in_=heads[:, :, :, ROTARY_DIM:HEAD_DIM],
+                )
+                add = nc.vector.tensor_tensor if (kind, half) == (KEY, 1) else nc.gpsimd.tensor_tensor
+                add(out=rotary, in0=rotary, in1=odd_share[:], op=ALU.add)
                 store(out, half, result)

@@ -26,7 +26,7 @@ UNIT_HEADS = UNIT_SHARDS * BLOCK // HEAD_DIM
 PACK = 4
 SCALE_ROWS = 4
 
-WARM_BEFORE, WARM_AFTER = 5, 2
+WARM_BEFORE, WARM_AFTER = 3, 2
 
 FLOPS = 2 * BATCH * SEQ * E * 3 * E
 
@@ -46,11 +46,11 @@ def tile_ttcodegenattention_pa_s_kernel(
 
         zeros = keep.tile([P, P], F32)
         nc.gpsimd.memset(zeros[:], 0.0)
-        last_bank = psum.tile([P, 2, UNIT_SHARDS, BLOCK], F32, name="bank_%d_%d" % (KEY, 1))
+        idle_bank = psum.tile([P, 2, UNIT_SHARDS, BLOCK], F32, name="bank_%d_%d" % (QUERY, 1))
 
         def idle_matmuls(count):
             for unused in range(count):
-                nc.tensor.matmul(out=last_bank[:, 0, 0, :], lhsT=zeros[:], rhs=zeros[:], start=True, stop=True)
+                nc.tensor.matmul(out=idle_bank[:, 0, 0, :], lhsT=zeros[:], rhs=zeros[:], start=True, stop=True)
 
         idle_matmuls(WARM_BEFORE)
 
@@ -130,42 +130,36 @@ def tile_ttcodegenattention_pa_s_kernel(
                 scales=x_scales[:, par, :],
                 in_=x_grouped[:, par].rearrange("p m t -> p (m t)"),
             )
-        factor = keep.tile([P, 2, 2, ROT_PAIRS, 2], F32)
-        nc.scalar.activation(
-            out=factor[:].rearrange("p par src i dst -> p (par src i dst)"),
-            in_=part[:],
-            func=ACT.Sin,
-            scale=2.0 * math.pi,
-        )
 
-        def project(kind, half, name):
-            bank = last_bank if (kind, half) == (KEY, 1) else psum.tile([P, 2, UNIT_SHARDS, BLOCK], F32, name=name)
-            for par in range(2):
-                for s in range(UNIT_SHARDS):
-                    col = (3 * (UNIT_SHARDS * half + s) + kind) * BLOCK
-                    nc.tensor.matmul_mx(
-                        out=bank[:, par, s, :],
-                        lhsT=x_codes[:, par, :].bitcast(FP8X4),
-                        lhsT_scale=x_scales[:, par, :],
-                        rhs=w_words[:, 2 * col : 2 * (col + BLOCK)].bitcast(FP4X4),
-                        rhs_scale=w_scales[:, col : col + BLOCK],
-                        start=True,
-                        stop=True,
-                    )
-            return bank
-
-        banks = {}
-        for kind in (VALUE, QUERY, KEY):
-            for half in range(2):
-                banks[(kind, half)] = project(kind, half, "bank_%d_%d" % (kind, half))
-
-        def empty(copy, bank, name):
-            result = keep.tile([P, UNIT_HEADS, 2, HEAD_DIM], F32, name=name)
-            copy(
-                out=result[:].rearrange("p h par d -> p par h d"),
-                in_=bank[:].rearrange("p par s (h d) -> p par (s h) d", d=HEAD_DIM),
+        def project(out, par, kind, shard):
+            col = (3 * shard + kind) * BLOCK
+            nc.tensor.matmul_mx(
+                out=out,
+                lhsT=x_codes[:, par, :].bitcast(FP8X4),
+                lhsT_scale=x_scales[:, par, :],
+                rhs=w_words[:, 2 * col : 2 * (col + BLOCK)].bitcast(FP4X4),
+                rhs_scale=w_scales[:, col : col + BLOCK],
+                start=True,
+                stop=True,
             )
-            return result
+
+        value_banks = []
+        for shard in range(2 * UNIT_SHARDS):
+            bank = psum.tile([P, 2, BLOCK], F32, name="bank_%d_%d" % (VALUE, shard))
+            for par in range(2):
+                project(bank[:, par, :], par, VALUE, shard)
+            value_banks.append(bank)
+        banks = {
+            (QUERY, 0): psum.tile([P, 2, UNIT_SHARDS, BLOCK], F32, name="bank_%d_%d" % (QUERY, 0)),
+            (QUERY, 1): idle_bank,
+            (KEY, 0): psum.tile([P, 2, UNIT_SHARDS, BLOCK], F32, name="x_t0"),
+            (KEY, 1): psum.tile([P, 2, UNIT_SHARDS, BLOCK], F32, name="x_t1"),
+        }
+        for kind in (QUERY, KEY):
+            for half in range(2):
+                for par in range(2):
+                    for s in range(UNIT_SHARDS):
+                        project(banks[(kind, half)][:, par, s, :], par, kind, UNIT_SHARDS * half + s)
 
         def store(out, half, result):
             heads = slice(UNIT_HEADS * half, UNIT_HEADS * (half + 1))
@@ -175,8 +169,23 @@ def tile_ttcodegenattention_pa_s_kernel(
                     in_=result[b:P:BATCH].rearrange("p h par d -> p h (par d)"),
                 )
 
-        store(out_2, 0, empty(nc.scalar.copy, banks[(VALUE, 0)], "v_0"))
-        store(out_2, 1, empty(nc.vector.tensor_copy, banks[(VALUE, 1)], "v_1"))
+        shard_heads = BLOCK // HEAD_DIM
+        factor = keep.tile([P, 2, 2, ROT_PAIRS, 2], F32)
+        for half in range(2):
+            result = keep.tile([P, UNIT_HEADS, 2, HEAD_DIM], F32, name="v_%d" % half)
+            for s, copy in ((0, nc.scalar.copy), (1, nc.vector.tensor_copy)):
+                copy(
+                    out=result[:, shard_heads * s : shard_heads * (s + 1)].rearrange("p h par d -> p par h d"),
+                    in_=value_banks[UNIT_SHARDS * half + s][:].rearrange("p par (h d) -> p par h d", d=HEAD_DIM),
+                )
+            store(out_2, half, result)
+            if half == 0:
+                nc.scalar.activation(
+                    out=factor[:].rearrange("p par src i dst -> p (par src i dst)"),
+                    in_=part[:],
+                    func=ACT.Sin,
+                    scale=2.0 * math.pi,
+                )
 
         shape = [P, 2, UNIT_HEADS, ROT_PAIRS, 2]
         for kind, out in ((QUERY, out_0), (KEY, out_1)):

@@ -32,8 +32,6 @@ FLOPS = 2 * BATCH * SEQ * E * 3 * E
 
 ROUND = 12582912.0
 
-SINE_FORM = (((1.0, 0.25), (1.0, 0.0)), ((-1.0, 0.0), (1.0, 0.25)))
-
 
 def tile_ttcodegenattention_pa_s_kernel(
     tc, hidden_states, w_qkv_words, w_qkv_scales, out_0, out_1, out_2
@@ -46,7 +44,7 @@ def tile_ttcodegenattention_pa_s_kernel(
 
         zeros = keep.tile([P, P], F32)
         nc.gpsimd.memset(zeros[:], 0.0)
-        idle_bank = psum.tile([P, 2, UNIT_SHARDS, BLOCK], F32, name="bank_%d_%d" % (QUERY, 1))
+        idle_bank = psum.tile([P, 2, UNIT_SHARDS, BLOCK], F32, name="bank_%d_%d" % (QUERY, 0))
 
         def idle_matmuls(count):
             for unused in range(count):
@@ -60,11 +58,11 @@ def tile_ttcodegenattention_pa_s_kernel(
             nc.sync.dma_start(out=x_sb[:, par, :], in_=x_by_par[par])
 
         w_scales = keep.tile([P, 3 * E], U8, align_bytes=64)
-        nc.vector.memset(w_scales[:].bitcast(I32), 0)
         for quadrant in range(4):
+            rows = w_qkv_scales[0, SCALE_ROWS * quadrant : SCALE_ROWS * (quadrant + 1), :].bitcast(I32)
             nc.sync.dma_start(
-                out=w_scales[32 * quadrant : 32 * quadrant + SCALE_ROWS, :].bitcast(I32),
-                in_=w_qkv_scales[0, SCALE_ROWS * quadrant : SCALE_ROWS * (quadrant + 1), :].bitcast(I32),
+                out=w_scales[32 * quadrant : 32 * (quadrant + 1), :].bitcast(I32),
+                in_=rows.unsqueeze(0).to_broadcast([32 // SCALE_ROWS, SCALE_ROWS, 3 * E // 4]),
             )
         w_words = keep.tile([P, 2 * 3 * E], U8, align_bytes=64)
         nc.sync.dma_start(out=w_words[:].bitcast(I32), in_=w_qkv_words[0].bitcast(I32))
@@ -84,29 +82,20 @@ def tile_ttcodegenattention_pa_s_kernel(
         nc.vector.tensor_single_scalar(out=even_pos[:], in_=lane[:], scalar=P - 2, op=ALU.bitwise_and)
         pos = keep.tile([P, 2], F32)
         nc.vector.tensor_tensor(out=pos[:], in0=even_pos[:], in1=par_bit[:], op=ALU.add)
-        turns = keep.tile([P, 2, ROT_PAIRS], F32)
+        phase = keep.tile([P, 3, ROT_PAIRS, 2], F32)
         for i in range(ROT_PAIRS):
             per_position = 1.0 / (ROPE_BASE ** (2.0 * i / ROTARY_DIM)) / (2.0 * math.pi)
-            nc.vector.tensor_scalar_mul(out=turns[:, :, i], in0=pos[:], scalar1=per_position)
-        phase = keep.tile([P, 2, 2, ROT_PAIRS, 2], F32)
-        for src in range(2):
-            for dst in range(2):
-                sign, shift = SINE_FORM[src][dst]
-                nc.vector.tensor_scalar(
-                    out=phase[:, :, src, :, dst],
-                    in0=turns[:],
-                    scalar1=sign,
-                    scalar2=shift,
-                    op0=ALU.mult,
-                    op1=ALU.add,
-                )
-        phase_flat = phase[:].rearrange("p par src i dst -> p (par src i dst)")
-        whole = keep.tile([P, 2 * 2 * ROTARY_DIM], F32)
+            nc.vector.tensor_scalar_mul(out=phase[:, 2, i, :], in0=pos[:], scalar1=per_position)
+        planes = phase[:].rearrange("p f i par -> p f (i par)")
+        nc.vector.tensor_scalar_add(out=planes[:, 1], in0=planes[:, 2], scalar1=0.25)
+        whole = keep.tile([P, 2, 2 * ROT_PAIRS], F32)
         nc.vector.tensor_scalar(
-            out=whole[:], in0=phase_flat, scalar1=ROUND, scalar2=ROUND, op0=ALU.add, op1=ALU.subtract
+            out=whole[:], in0=planes[:, 1:3], scalar1=ROUND, scalar2=ROUND, op0=ALU.add, op1=ALU.subtract
         )
-        part = keep.tile([P, 2 * 2 * ROTARY_DIM], F32)
-        nc.vector.tensor_tensor(out=part[:], in0=phase_flat, in1=whole[:], op=ALU.subtract)
+        part = keep.tile([P, 3, ROT_PAIRS, 2], F32)
+        parts = part[:].rearrange("p f i par -> p f (i par)")
+        nc.vector.tensor_tensor(out=parts[:, 1:3], in0=planes[:, 1:3], in1=whole[:], op=ALU.subtract)
+        nc.vector.tensor_scalar_mul(out=parts[:, 0], in0=parts[:, 2], scalar1=-1.0)
 
         x_grouped = keep.tile([P, 2, P, PACK], BF16, align_bytes=64)
         x_codes = keep.tile([P, 2, P], U32, align_bytes=64)
@@ -116,7 +105,8 @@ def tile_ttcodegenattention_pa_s_kernel(
             x_t = psum.tile([P, 2, P], F32, name="x_t%d" % par)
             for u in range(2):
                 nc.tensor.transpose(x_t[:, u, :], x_words[:, u : E // 2 : 2], identity[:])
-            nc.scalar.copy(
+            copy = nc.scalar.copy if par == 0 else nc.vector.tensor_copy
+            copy(
                 out=x_grouped[:, par]
                 .rearrange("p m t -> p (m t)")
                 .bitcast(F32)
@@ -124,6 +114,14 @@ def tile_ttcodegenattention_pa_s_kernel(
                 in_=x_t[:].rearrange("p u m -> p m u"),
             )
         idle_matmuls(WARM_AFTER)
+        factor = keep.tile([P, 2, 2, ROT_PAIRS, 2], F32)
+        for src in range(2):
+            nc.scalar.activation(
+                out=factor[:, :, src],
+                in_=part[:, 1 - src : 3 - src].rearrange("p dst i par -> p par i dst"),
+                func=ACT.Sin,
+                scale=2.0 * math.pi,
+            )
         for par in range(2):
             nc.vector.quantize_mx(
                 out=x_codes[:, par, :].bitcast(FP8X4),
@@ -143,15 +141,42 @@ def tile_ttcodegenattention_pa_s_kernel(
                 stop=True,
             )
 
-        value_banks = []
-        for shard in range(2 * UNIT_SHARDS):
+        first_banks = []
+        for par in range(2):
+            bank = psum.tile([P, BLOCK], F32, name="first_%d" % par)
+            project(bank[:], par, VALUE, 0)
+            first_banks.append(bank)
+        value_banks = {}
+        for shard in range(1, 2 * UNIT_SHARDS):
             bank = psum.tile([P, 2, BLOCK], F32, name="bank_%d_%d" % (VALUE, shard))
             for par in range(2):
                 project(bank[:, par, :], par, VALUE, shard)
-            value_banks.append(bank)
+            value_banks[shard] = bank
+        def store(out, first_head, result):
+            heads = slice(first_head, first_head + result.shape[1])
+            for b in range(BATCH):
+                nc.sync.dma_start(
+                    out=out[b, heads].rearrange("h (pair par) d -> pair h (par d)", par=2),
+                    in_=result[b:P:BATCH].rearrange("p h par d -> p h (par d)"),
+                )
+
+        shard_heads = BLOCK // HEAD_DIM
+        result = keep.tile([P, shard_heads, 2, HEAD_DIM], F32, name="v_first")
+        for par, copy in ((0, nc.scalar.copy), (1, nc.vector.tensor_copy)):
+            copy(out=result[:, :, par, :], in_=first_banks[par][:].rearrange("p (h d) -> p h d", d=HEAD_DIM))
+        store(out_2, 0, result)
+        for shards in ((1,), (2, 3)):
+            result = keep.tile([P, shard_heads * len(shards), 2, HEAD_DIM], F32, name="v_%d" % shards[0])
+            for s, shard in enumerate(shards):
+                nc.scalar.copy(
+                    out=result[:, shard_heads * s : shard_heads * (s + 1)].rearrange("p h par d -> p par h d"),
+                    in_=value_banks[shard][:].rearrange("p par (h d) -> p par h d", d=HEAD_DIM),
+                )
+            store(out_2, shard_heads * shards[0], result)
+
         banks = {
-            (QUERY, 0): psum.tile([P, 2, UNIT_SHARDS, BLOCK], F32, name="bank_%d_%d" % (QUERY, 0)),
-            (QUERY, 1): idle_bank,
+            (QUERY, 0): idle_bank,
+            (QUERY, 1): psum.tile([P, 2, UNIT_SHARDS, BLOCK], F32, name="first_0"),
             (KEY, 0): psum.tile([P, 2, UNIT_SHARDS, BLOCK], F32, name="x_t0"),
             (KEY, 1): psum.tile([P, 2, UNIT_SHARDS, BLOCK], F32, name="x_t1"),
         }
@@ -160,32 +185,6 @@ def tile_ttcodegenattention_pa_s_kernel(
                 for par in range(2):
                     for s in range(UNIT_SHARDS):
                         project(banks[(kind, half)][:, par, s, :], par, kind, UNIT_SHARDS * half + s)
-
-        def store(out, half, result):
-            heads = slice(UNIT_HEADS * half, UNIT_HEADS * (half + 1))
-            for b in range(BATCH):
-                nc.sync.dma_start(
-                    out=out[b, heads].rearrange("h (pair par) d -> pair h (par d)", par=2),
-                    in_=result[b:P:BATCH].rearrange("p h par d -> p h (par d)"),
-                )
-
-        shard_heads = BLOCK // HEAD_DIM
-        factor = keep.tile([P, 2, 2, ROT_PAIRS, 2], F32)
-        for half in range(2):
-            result = keep.tile([P, UNIT_HEADS, 2, HEAD_DIM], F32, name="v_%d" % half)
-            for s, copy in ((0, nc.scalar.copy), (1, nc.vector.tensor_copy)):
-                copy(
-                    out=result[:, shard_heads * s : shard_heads * (s + 1)].rearrange("p h par d -> p par h d"),
-                    in_=value_banks[UNIT_SHARDS * half + s][:].rearrange("p par (h d) -> p par h d", d=HEAD_DIM),
-                )
-            store(out_2, half, result)
-            if half == 0:
-                nc.scalar.activation(
-                    out=factor[:].rearrange("p par src i dst -> p (par src i dst)"),
-                    in_=part[:],
-                    func=ACT.Sin,
-                    scale=2.0 * math.pi,
-                )
 
         shape = [P, 2, UNIT_HEADS, ROT_PAIRS, 2]
         for kind, out in ((QUERY, out_0), (KEY, out_1)):
@@ -209,4 +208,4 @@ def tile_ttcodegenattention_pa_s_kernel(
                 )
                 add = nc.vector.tensor_tensor if (kind, half) == (KEY, 1) else nc.gpsimd.tensor_tensor
                 add(out=rotary, in0=rotary, in1=odd_share[:], op=ALU.add)
-                store(out, half, result)
+                store(out, UNIT_HEADS * half, result)

@@ -58,11 +58,11 @@ def tile_ttcodegenattention_pa_s_kernel(
             nc.sync.dma_start(out=x_sb[:, par, :], in_=x_by_par[par])
 
         w_scales = keep.tile([P, 3 * E], U8, align_bytes=64)
+        nc.vector.memset(w_scales[:].bitcast(I32), 0)
         for quadrant in range(4):
-            rows = w_qkv_scales[0, SCALE_ROWS * quadrant : SCALE_ROWS * (quadrant + 1), :].bitcast(I32)
             nc.sync.dma_start(
-                out=w_scales[32 * quadrant : 32 * (quadrant + 1), :].bitcast(I32),
-                in_=rows.unsqueeze(0).to_broadcast([32 // SCALE_ROWS, SCALE_ROWS, 3 * E // 4]),
+                out=w_scales[32 * quadrant : 32 * quadrant + SCALE_ROWS, :].bitcast(I32),
+                in_=w_qkv_scales[0, SCALE_ROWS * quadrant : SCALE_ROWS * (quadrant + 1), :].bitcast(I32),
             )
         w_words = keep.tile([P, 2 * 3 * E], U8, align_bytes=64)
         nc.sync.dma_start(out=w_words[:].bitcast(I32), in_=w_qkv_words[0].bitcast(I32))

@@ -32,6 +32,8 @@ FLOPS = 2 * BATCH * SEQ * E * 3 * E
 
 ROUND = 12582912.0
 
+SINE_FORM = (((1.0, 0.25), (1.0, 0.0)), ((-1.0, 0.0), (1.0, 0.25)))
+
 
 def tile_ttcodegenattention_pa_s_kernel(
     tc, hidden_states, w_qkv_words, w_qkv_scales, out_0, out_1, out_2
@@ -82,20 +84,29 @@ def tile_ttcodegenattention_pa_s_kernel(
         nc.vector.tensor_single_scalar(out=even_pos[:], in_=lane[:], scalar=P - 2, op=ALU.bitwise_and)
         pos = keep.tile([P, 2], F32)
         nc.vector.tensor_tensor(out=pos[:], in0=even_pos[:], in1=par_bit[:], op=ALU.add)
-        phase = keep.tile([P, 3, ROT_PAIRS, 2], F32)
+        turns = keep.tile([P, 2, ROT_PAIRS], F32)
         for i in range(ROT_PAIRS):
             per_position = 1.0 / (ROPE_BASE ** (2.0 * i / ROTARY_DIM)) / (2.0 * math.pi)
-            nc.vector.tensor_scalar_mul(out=phase[:, 2, i, :], in0=pos[:], scalar1=per_position)
-        planes = phase[:].rearrange("p f i par -> p f (i par)")
-        nc.vector.tensor_scalar_add(out=planes[:, 1], in0=planes[:, 2], scalar1=0.25)
-        whole = keep.tile([P, 2, 2 * ROT_PAIRS], F32)
+            nc.vector.tensor_scalar_mul(out=turns[:, :, i], in0=pos[:], scalar1=per_position)
+        phase = keep.tile([P, 2, 2, ROT_PAIRS, 2], F32)
+        for src in range(2):
+            for dst in range(2):
+                sign, shift = SINE_FORM[src][dst]
+                nc.vector.tensor_scalar(
+                    out=phase[:, :, src, :, dst],
+                    in0=turns[:],
+                    scalar1=sign,
+                    scalar2=shift,
+                    op0=ALU.mult,
+                    op1=ALU.add,
+                )
+        phase_flat = phase[:].rearrange("p par src i dst -> p (par src i dst)")
+        whole = keep.tile([P, 2 * 2 * ROTARY_DIM], F32)
         nc.vector.tensor_scalar(
-            out=whole[:], in0=planes[:, 1:3], scalar1=ROUND, scalar2=ROUND, op0=ALU.add, op1=ALU.subtract
+            out=whole[:], in0=phase_flat, scalar1=ROUND, scalar2=ROUND, op0=ALU.add, op1=ALU.subtract
         )
-        part = keep.tile([P, 3, ROT_PAIRS, 2], F32)
-        parts = part[:].rearrange("p f i par -> p f (i par)")
-        nc.vector.tensor_tensor(out=parts[:, 1:3], in0=planes[:, 1:3], in1=whole[:], op=ALU.subtract)
-        nc.vector.tensor_scalar_mul(out=parts[:, 0], in0=parts[:, 2], scalar1=-1.0)
+        part = keep.tile([P, 2 * 2 * ROTARY_DIM], F32)
+        nc.vector.tensor_tensor(out=part[:], in0=phase_flat, in1=whole[:], op=ALU.subtract)
 
         x_grouped = keep.tile([P, 2, P, PACK], BF16, align_bytes=64)
         x_codes = keep.tile([P, 2, P], U32, align_bytes=64)
@@ -105,8 +116,7 @@ def tile_ttcodegenattention_pa_s_kernel(
             x_t = psum.tile([P, 2, P], F32, name="x_t%d" % par)
             for u in range(2):
                 nc.tensor.transpose(x_t[:, u, :], x_words[:, u : E // 2 : 2], identity[:])
-            copy = nc.scalar.copy if par == 0 else nc.vector.tensor_copy
-            copy(
+            nc.scalar.copy(
                 out=x_grouped[:, par]
                 .rearrange("p m t -> p (m t)")
                 .bitcast(F32)
@@ -114,14 +124,6 @@ def tile_ttcodegenattention_pa_s_kernel(
                 in_=x_t[:].rearrange("p u m -> p m u"),
             )
         idle_matmuls(WARM_AFTER)
-        factor = keep.tile([P, 2, 2, ROT_PAIRS, 2], F32)
-        for src in range(2):
-            nc.scalar.activation(
-                out=factor[:, :, src],
-                in_=part[:, 1 - src : 3 - src].rearrange("p dst i par -> p par i dst"),
-                func=ACT.Sin,
-                scale=2.0 * math.pi,
-            )
         for par in range(2):
             nc.vector.quantize_mx(
                 out=x_codes[:, par, :].bitcast(FP8X4),
@@ -165,6 +167,13 @@ def tile_ttcodegenattention_pa_s_kernel(
         for par, copy in ((0, nc.scalar.copy), (1, nc.vector.tensor_copy)):
             copy(out=result[:, :, par, :], in_=first_banks[par][:].rearrange("p (h d) -> p h d", d=HEAD_DIM))
         store(out_2, 0, result)
+        factor = keep.tile([P, 2, 2, ROT_PAIRS, 2], F32)
+        nc.scalar.activation(
+            out=factor[:].rearrange("p par src i dst -> p (par src i dst)"),
+            in_=part[:],
+            func=ACT.Sin,
+            scale=2.0 * math.pi,
+        )
         for shards in ((1,), (2, 3)):
             result = keep.tile([P, shard_heads * len(shards), 2, HEAD_DIM], F32, name="v_%d" % shards[0])
             for s, shard in enumerate(shards):

import math
from contextlib import ExitStack

import concourse.mybir as mybir
from concourse.masks import make_identity

F32 = mybir.dt.float32
BF16 = mybir.dt.bfloat16
I32 = mybir.dt.int32
U32 = mybir.dt.uint32
U8 = mybir.dt.uint8
FP8X4 = mybir.dt.float8_e4m3fn_x4
FP4X4 = mybir.dt.float4_e2m1fn_x4
ALU = mybir.AluOpType
ACT = mybir.ActivationFunctionType

P = 128
BATCH, SEQ, E = 2, 128, 512
HEAD_DIM, ROTARY_DIM = 32, 16
ROT_PAIRS = ROTARY_DIM // 2
ROPE_BASE = 10000.0
BLOCK = 128
QUERY, VALUE, KEY = 0, 1, 2
UNIT_SHARDS = 2
UNIT_HEADS = UNIT_SHARDS * BLOCK // HEAD_DIM
PACK = 4
SCALE_ROWS = 4

WARM_BEFORE, WARM_AFTER = 3, 2

FLOPS = 2 * BATCH * SEQ * E * 3 * E

ROUND = 12582912.0

SINE_FORM = (((1.0, 0.25), (1.0, 0.0)), ((-1.0, 0.0), (1.0, 0.25)))


def tile_ttcodegenattention_pa_s_kernel(
    tc, hidden_states, w_qkv_words, w_qkv_scales, out_0, out_1, out_2
):
    nc = tc.nc
    with ExitStack() as ctx:
        keep = ctx.enter_context(tc.tile_pool(name="keep", bufs=1))
        psum = ctx.enter_context(tc.psum_pool(name="psum", bufs=1))
        ctx.enter_context(tc.manual_schedule())

        zeros = keep.tile([P, P], F32)
        nc.gpsimd.memset(zeros[:], 0.0)
        idle_bank = psum.tile([P, 2, UNIT_SHARDS, BLOCK], F32, name="bank_%d_%d" % (QUERY, 0))

        def idle_matmuls(count):
            for unused in range(count):
                nc.tensor.matmul(out=idle_bank[:, 0, 0, :], lhsT=zeros[:], rhs=zeros[:], start=True, stop=True)

        idle_matmuls(WARM_BEFORE)

        x_sb = keep.tile([P, 2, E], BF16)
        x_by_par = hidden_states.rearrange("b (pair par) k -> par pair b k", par=2)
        for par in range(2):
            nc.sync.dma_start(out=x_sb[:, par, :], in_=x_by_par[par])

        w_scales = keep.tile([P, 3 * E], U8, align_bytes=64)
        nc.vector.memset(w_scales[:].bitcast(I32), 0)
        for quadrant in range(4):
            nc.sync.dma_start(
                out=w_scales[32 * quadrant : 32 * quadrant + SCALE_ROWS, :].bitcast(I32),
                in_=w_qkv_scales[0, SCALE_ROWS * quadrant : SCALE_ROWS * (quadrant + 1), :].bitcast(I32),
            )
        w_words = keep.tile([P, 2 * 3 * E], U8, align_bytes=64)
        nc.sync.dma_start(out=w_words[:].bitcast(I32), in_=w_qkv_words[0].bitcast(I32))

        warm = keep.tile([P, 1], F32)
        nc.vector.memset(warm[:], 0.0)
        nc.scalar.activation(out=warm[:], in_=warm[:], func=ACT.Sin)

        lane = keep.tile([P, 2], I32)
        nc.gpsimd.iota(lane[:], pattern=[[0, 2]], base=0, channel_multiplier=1)
        par_bit = keep.tile([P, 2], I32)
        nc.gpsimd.iota(par_bit[:], pattern=[[1, 2]], base=0, channel_multiplier=0)
        identity = keep.tile([P, P], F32)
        make_identity(nc, identity[:])

        even_pos = keep.tile([P, 2], I32)
        nc.vector.tensor_single_scalar(out=even_pos[:], in_=lane[:], scalar=P - 2, op=ALU.bitwise_and)
        pos = keep.tile([P, 2], F32)
        nc.vector.tensor_tensor(out=pos[:], in0=even_pos[:], in1=par_bit[:], op=ALU.add)
        turns = keep.tile([P, 2, ROT_PAIRS], F32)
        for i in range(ROT_PAIRS):
            per_position = 1.0 / (ROPE_BASE ** (2.0 * i / ROTARY_DIM)) / (2.0 * math.pi)
            nc.vector.tensor_scalar_mul(out=turns[:, :, i], in0=pos[:], scalar1=per_position)
        phase = keep.tile([P, 2, 2, ROT_PAIRS, 2], F32)
        for src in range(2):
            for dst in range(2):
                sign, shift = SINE_FORM[src][dst]
                nc.vector.tensor_scalar(
                    out=phase[:, :, src, :, dst],
                    in0=turns[:],
                    scalar1=sign,
                    scalar2=shift,
                    op0=ALU.mult,
                    op1=ALU.add,
                )
        phase_flat = phase[:].rearrange("p par src i dst -> p (par src i dst)")
        whole = keep.tile([P, 2 * 2 * ROTARY_DIM], F32)
        nc.vector.tensor_scalar(
            out=whole[:], in0=phase_flat, scalar1=ROUND, scalar2=ROUND, op0=ALU.add, op1=ALU.subtract
        )
        part = keep.tile([P, 2 * 2 * ROTARY_DIM], F32)
        nc.vector.tensor_tensor(out=part[:], in0=phase_flat, in1=whole[:], op=ALU.subtract)

        x_grouped = keep.tile([P, 2, P, PACK], BF16, align_bytes=64)
        x_codes = keep.tile([P, 2, P], U32, align_bytes=64)
        x_scales = keep.tile([P, 2, P], U8, align_bytes=64)
        for par in range(2):
            x_words = x_sb[:, par, :].bitcast(F32)
            x_t = psum.tile([P, 2, P], F32, name="x_t%d" % par)
            for u in range(2):
                nc.tensor.transpose(x_t[:, u, :], x_words[:, u : E // 2 : 2], identity[:])
            nc.scalar.copy(
                out=x_grouped[:, par]
                .rearrange("p m t -> p (m t)")
                .bitcast(F32)
                .rearrange("p (m u) -> p m u", u=2),
                in_=x_t[:].rearrange("p u m -> p m u"),
            )
        idle_matmuls(WARM_AFTER)
        for par in range(2):
            nc.vector.quantize_mx(
                out=x_codes[:, par, :].bitcast(FP8X4),
                scales=x_scales[:, par, :],
                in_=x_grouped[:, par].rearrange("p m t -> p (m t)"),
            )

        def project(out, par, kind, shard):
            col = (3 * shard + kind) * BLOCK
            nc.tensor.matmul_mx(
                out=out,
                lhsT=x_codes[:, par, :].bitcast(FP8X4),
                lhsT_scale=x_scales[:, par, :],
                rhs=w_words[:, 2 * col : 2 * (col + BLOCK)].bitcast(FP4X4),
                rhs_scale=w_scales[:, col : col + BLOCK],
                start=True,
                stop=True,
            )

        first_banks = []
        for par in range(2):
            bank = psum.tile([P, BLOCK], F32, name="first_%d" % par)
            project(bank[:], par, VALUE, 0)
            first_banks.append(bank)
        value_banks = {}
        for shard in range(1, 2 * UNIT_SHARDS):
            bank = psum.tile([P, 2, BLOCK], F32, name="bank_%d_%d" % (VALUE, shard))
            for par in range(2):
                project(bank[:, par, :], par, VALUE, shard)
            value_banks[shard] = bank
        def store(out, first_head, result):
            heads = slice(first_head, first_head + result.shape[1])
            for b in range(BATCH):
                nc.sync.dma_start(
                    out=out[b, heads].rearrange("h (pair par) d -> pair h (par d)", par=2),
                    in_=result[b:P:BATCH].rearrange("p h par d -> p h (par d)"),
                )

        shard_heads = BLOCK // HEAD_DIM
        result = keep.tile([P, shard_heads, 2, HEAD_DIM], F32, name="v_first")
        for par, copy in ((0, nc.scalar.copy), (1, nc.vector.tensor_copy)):
            copy(out=result[:, :, par, :], in_=first_banks[par][:].rearrange("p (h d) -> p h d", d=HEAD_DIM))
        store(out_2, 0, result)
        factor = keep.tile([P, 2, 2, ROT_PAIRS, 2], F32)
        nc.scalar.activation(
            out=factor[:].rearrange("p par src i dst -> p (par src i dst)"),
            in_=part[:],
            func=ACT.Sin,
            scale=2.0 * math.pi,
        )
        for shards in ((1,), (2, 3)):
            result = keep.tile([P, shard_heads * len(shards), 2, HEAD_DIM], F32, name="v_%d" % shards[0])
            for s, shard in enumerate(shards):
                nc.scalar.copy(
                    out=result[:, shard_heads * s : shard_heads * (s + 1)].rearrange("p h par d -> p par h d"),
                    in_=value_banks[shard][:].rearrange("p par (h d) -> p par h d", d=HEAD_DIM),
                )
            store(out_2, shard_heads * shards[0], result)

        banks = {
            (QUERY, 0): idle_bank,
            (QUERY, 1): psum.tile([P, 2, UNIT_SHARDS, BLOCK], F32, name="first_0"),
            (KEY, 0): psum.tile([P, 2, UNIT_SHARDS, BLOCK], F32, name="x_t0"),
            (KEY, 1): psum.tile([P, 2, UNIT_SHARDS, BLOCK], F32, name="x_t1"),
        }
        for kind in (QUERY, KEY):
            for half in range(2):
                for par in range(2):
                    for s in range(UNIT_SHARDS):
                        project(banks[(kind, half)][:, par, s, :], par, kind, UNIT_SHARDS * half + s)

        shape = [P, 2, UNIT_HEADS, ROT_PAIRS, 2]
        for kind, out in ((QUERY, out_0), (KEY, out_1)):
            for half in range(2):
                bank = banks[(kind, half)]
                result = keep.tile([P, UNIT_HEADS, 2, HEAD_DIM], F32, name="qk_%d_%d" % (kind, half))
                rotary = result[:, :, :, 0:ROTARY_DIM]
                odd_share = keep.tile([P, UNIT_HEADS, 2, ROTARY_DIM], F32, name="odd_%d_%d" % (kind, half))
                heads = bank[:].rearrange("p par s (h d) -> p par (s h) d", d=HEAD_DIM)
                pairs = heads[:, :, :, 0:ROTARY_DIM].rearrange("p par h (i e) -> p par h i e", e=2)
                for src, share in ((0, rotary), (1, odd_share[:])):
                    nc.vector.tensor_tensor(
                        out=share.rearrange("p h par (i e) -> p par h i e", e=2),
                        in0=pairs[:, :, :, :, src : src + 1].to_broadcast(shape),
                        in1=factor[:, :, src].unsqueeze(2).to_broadcast(shape),
                        op=ALU.mult,
                    )
                nc.scalar.copy(
                    out=result[:, :, :, ROTARY_DIM:HEAD_DIM].rearrange("p h par d -> p par h d"),
                    in_=heads[:, :, :, ROTARY_DIM:HEAD_DIM],
                )
                add = nc.vector.tensor_tensor if (kind, half) == (KEY, 1) else nc.gpsimd.tensor_tensor
                add(out=rotary, in0=rotary, in1=odd_share[:], op=ALU.add)
                store(out, UNIT_HEADS * half, result)
